import numpy as np
import ml_dtypes


BF16 = ml_dtypes.bfloat16


def bf(x):
    return np.asarray(x, np.float32).astype(BF16)


def f64(x):
    return np.asarray(x).astype(np.float64)


E2M1 = np.array([0.0, 0.5, 1.0, 1.5, 2.0, 3.0, 4.0, 6.0, -0.0, -0.5, -1.0, -1.5, -2.0, -3.0, -4.0, -6.0])


def pack_weight(w, fmt):
    k, n = w.shape
    w = f64(bf(w)).reshape(k // 32, 32, n)
    amax = np.abs(w).max(1)
    if fmt == "e4m3":
        byte = np.frexp(amax)[1] - 1 + 127 - 7
    else:
        mant, ex = np.frexp(amax / 6.0)
        byte = np.where(mant > 0.5, ex, ex - 1) + 127
    byte = np.clip(np.where(amax > 0, byte, 1), 1, 254)
    scaled = (w * np.exp2(127.0 - byte)[:, None, :]).reshape(k, n).astype(np.float32)
    by_word = np.ascontiguousarray(scaled.reshape(k // 512, 128, 4, n).transpose(0, 1, 3, 2))
    if fmt == "e4m3":
        words = by_word.astype(ml_dtypes.float8_e4m3fn).view(np.uint8)
    else:
        c = by_word.astype(ml_dtypes.float4_e2m1fn).view(np.uint8) & 0xF
        words = c[..., 0::2] | (c[..., 1::2] << 4)
    return np.ascontiguousarray(words), np.ascontiguousarray(byte.astype(np.uint8).reshape(k // 512, 16, n))


def unpack_weight(words, scales, fmt):
    g, p, n, _ = words.shape
    if fmt == "e4m3":
        vals = np.ascontiguousarray(words).view(ml_dtypes.float8_e4m3fn).astype(np.float64)
    else:
        nib = np.empty((g, p, n, 4), np.uint8)
        nib[..., 0::2] = words & 0xF
        nib[..., 1::2] = words >> 4
        vals = E2M1[nib]
    vals = vals * np.repeat(np.exp2(scales.astype(np.float64) - 127.0), 8, axis=1)[..., None]
    return vals.transpose(0, 1, 3, 2).reshape(g * 512, n)

def pack4(w):
    words, scales = pack_weight(w, "e2m1")
    return words.reshape(words.shape[0], 128, -1), scales


def unpack4(words, scales):
    return unpack_weight(words.reshape(words.shape[0], 128, -1, 2), scales, "e2m1")


def kspread(k):
    return np.exp2(np.repeat(np.random.randint(-6, 7, k // 32), 32).astype(np.float64))


B, L, N, HID, H, D = 1, 128, 384, 3072, 12, 128


def apply_rope(x, rope):
    xp = x.reshape(x.shape[:-1] + (D // 2, 2))
    rp = rope[:, None].reshape(rope.shape[0], 1, rope.shape[1], D // 2, 2)
    cos, sin = rp[..., 0], rp[..., 1]
    x0, x1 = xp[..., 0], xp[..., 1]
    out = np.stack([x0 * cos - x1 * sin, x1 * cos + x0 * sin], axis=-1)
    return out.reshape(x.shape)


def setup_inputs():
    s = kspread(HID)
    img = np.random.standard_normal((B, N, HID)) * s
    img_words, img_scales = pack4(np.ascontiguousarray(img.reshape(B * N, HID).T))
    rope = bf(np.random.standard_normal((B, N, D)))
    w = np.random.standard_normal((3 * H * D, HID)) / np.sqrt(HID) / s
    words, scales = pack4(np.ascontiguousarray(w.T))
    return {"img_words": img_words,
            "img_scales": img_scales,
            "rope": rope,
            "W_img_qkv_words": words,
            "W_img_qkv_scales": scales}


def reference(img_words, img_scales, rope, W_img_qkv_words, W_img_qkv_scales):
    x = unpack4(img_words, img_scales).T.reshape(B, N, HID)
    y = x @ unpack4(W_img_qkv_words, W_img_qkv_scales)
    y = y.reshape(B, N, 3, H, D).transpose(2, 0, 3, 1, 4)
    r = f64(rope)
    return apply_rope(y[0], r), apply_rope(y[1], r), y[2]

@@ -1,0 +1,190 @@
+from contextlib import ExitStack
+
+import concourse.mybir as mybir
+
+P = 128
+TOKENS, K, COLS = 384, 3072, 4608
+HEADS, D = 12, 128
+PASSES = K // 512
+M_TILES = TOKENS // P
+N_TILE = 512
+HEADS_PER_TILE = N_TILE // D
+BLOCKS = COLS // N_TILE
+ROPE_BLOCKS = 6
+FLOPS = 2 * TOKENS * K * COLS
+
+GROUPS = ((0, 512), (512, 1024), (1536, 1536), (3072, 1536))
+
+F32 = mybir.dt.float32
+BF16 = mybir.dt.bfloat16
+I32 = mybir.dt.int32
+U8 = mybir.dt.uint8
+FP4X4 = mybir.dt.float4_e2m1fn_x4
+MULT = mybir.AluOpType.mult
+ADD = mybir.AluOpType.add
+
+
+def tile_jointattention_pa_kernel(
+    tc, img_words, img_scales, rope, w_words, w_scales, out_q, out_k, out_v
+):
+    nc = tc.nc
+    outs = (out_q, out_k, out_v)
+
+    with ExitStack() as ctx:
+        keep = ctx.enter_context(tc.tile_pool(name="keep", bufs=1))
+        work = ctx.enter_context(tc.tile_pool(name="work", bufs=4))
+        outp = ctx.enter_context(tc.tile_pool(name="outp", bufs=12))
+        psum = ctx.enter_context(tc.psum_pool(name="psum", bufs=8))
+        ctx.enter_context(tc.manual_schedule())
+
+        x_codes = keep.tile([P, PASSES, 2 * TOKENS], U8, align_bytes=256, name="x_codes")
+        x_planes = keep.tile([P, PASSES, TOKENS], U8, align_bytes=256, name="x_planes")
+        w_codes = []
+        w_planes = []
+        for i, (c0, width) in enumerate(GROUPS):
+            codes = keep.tile([P, PASSES, 2 * width], U8, align_bytes=256, name=f"w_codes{i}")
+            planes = keep.tile([P, PASSES, width], U8, align_bytes=256, name=f"w_planes{i}")
+            w_codes.append(codes)
+            w_planes.append(planes)
+        warm = keep.tile([P, N_TILE], BF16, name="warm")
+        warm_out = keep.tile([P, 1], BF16, name="warm_out")
+        rope_raw = keep.tile([P, M_TILES, D], BF16, name="rope_raw")
+        cos_t = keep.tile([P, M_TILES, D], F32, name="cos_t")
+        sin_t = keep.tile([P, M_TILES, D], F32, name="sin_t")
+
+        def load_x_codes(g0, g1):
+            nc.sync.dma_start(
+                out=x_codes[:, g0:g1, :].bitcast(I32),
+                in_=img_words[g0:g1].rearrange("g p n -> p g n").bitcast(I32),
+            )
+
+        def load_w_codes(i, g0, g1):
+            c0, width = GROUPS[i]
+            nc.sync.dma_start(
+                out=w_codes[i][:, g0:g1, :].bitcast(I32),
+                in_=w_words[g0:g1, :, 2 * c0 : 2 * (c0 + width)].rearrange("g p n -> p g n").bitcast(I32),
+            )
+
+        def load_planes(planes, scales, c0, width):
+            for q in range(4):
+                nc.sync.dma_start(
+                    out=planes[32 * q : 32 * q + 4, :, :].bitcast(I32),
+                    in_=scales[:, 4 * q : 4 * q + 4, c0 : c0 + width].rearrange("g r n -> r g n").bitcast(I32),
+                )
+
+        nc.vector.memset(warm[:], 0.0)
+        nc.vector.memset(x_planes[:].bitcast(I32), 0)
+        nc.vector.memset(w_planes[0][:].bitcast(I32), 0)
+        nc.vector.memset(w_planes[1][:].bitcast(I32), 0)
+        nc.gpsimd.dma_start(out=rope_raw[:], in_=rope[0].rearrange("(m p) d -> p m d", p=P))
+        nc.gpsimd.memset(w_planes[2][:].bitcast(I32), 0)
+        nc.gpsimd.memset(w_planes[3][:].bitcast(I32), 0)
+        nc.scalar.copy(out=warm_out[:], in_=warm[:, 0:1])
+
+        load_x_codes(0, 1)
+        load_w_codes(0, 0, 1)
+        load_planes(x_planes, img_scales, 0, TOKENS)
+        load_planes(w_planes[0], w_scales, 0, GROUPS[0][1])
+        load_x_codes(1, 3)
+        load_w_codes(0, 1, 3)
+        load_x_codes(3, 6)
+        load_w_codes(0, 3, 6)
+        for i in (1, 2):
+            load_planes(w_planes[i], w_scales, *GROUPS[i])
+            for g in range(0, PASSES, 2):
+                load_w_codes(i, g, g + 2)
+
+        raw = rope_raw[:].rearrange("p m (i t) -> p (m i) t", t=2)
+        cos_v = cos_t[:].rearrange("p m (i t) -> p (m i) t", t=2)
+        sin_v = sin_t[:].rearrange("p m (i t) -> p (m i) t", t=2)
+        nc.vector.tensor_copy(out=cos_v, in_=raw[:, :, 0:1].to_broadcast([P, M_TILES * D // 2, 2]))
+        nc.vector.tensor_scalar(out=sin_v[:, :, 0:1], in0=raw[:, :, 1:2], scalar1=-1.0, scalar2=None, op0=MULT)
+        nc.vector.tensor_copy(out=sin_v[:, :, 1:2], in_=raw[:, :, 1:2])
+
+        dummy = psum.tile([P, N_TILE], F32, name="bank")
+        for _ in range(12):
+            nc.tensor.matmul(dummy[:], lhsT=warm[:, :P], rhs=warm[:], start=True, stop=True)
+
+        def one_pass(bank, b, m, g, off=0, width=N_TILE):
+            i = max(j for j, (c0, w) in enumerate(GROUPS) if c0 <= b * N_TILE)
+            c = b * N_TILE - GROUPS[i][0] + off
+            nc.tensor.matmul_mx(
+                out=bank[:, :width],
+                lhsT=x_codes[:, g, 2 * P * m : 2 * P * (m + 1)].bitcast(FP4X4),
+                lhsT_scale=x_planes[:, g, P * m : P * (m + 1)],
+                rhs=w_codes[i][:, g, 2 * c : 2 * (c + width)].bitcast(FP4X4),
+                rhs_scale=w_planes[i][:, g, c : c + width],
+                start=(g == 0),
+                stop=(g == PASSES - 1),
+            )
+
+        def store(b, m, tile_ap, h_off, heads):
+            h0 = (b % 3) * HEADS_PER_TILE + h_off
+            nc.sync.dma_start(
+                out=outs[b // 3][0, h0 : h0 + heads, P * m : P * (m + 1), :].rearrange("h n d -> n h d"),
+                in_=tile_ap.rearrange("p (h d) -> p h d", d=D),
+            )
+
+        def rotate(b, m, bank):
+            shape = [P, HEADS_PER_TILE, D]
+            direct = work.tile([P, N_TILE], F32, name="direct")
+            crossed = work.tile([P, N_TILE], F32, name="crossed")
+            result = outp.tile([P, N_TILE], F32, name="result")
+            nc.vector.tensor_tensor(
+                out=direct[:].rearrange("p (h d) -> p h d", d=D),
+                in0=bank[:].rearrange("p (h d) -> p h d", d=D),
+                in1=cos_t[:, m : m + 1, :].to_broadcast(shape),
+                op=MULT,
+            )
+            nc.vector.tensor_tensor(
+                out=crossed[:].rearrange("p (h i t) -> p h i t", t=2, i=D // 2),
+                in0=bank[:].rearrange("p (h i t) -> p h i t", t=2, i=D // 2)[:, :, :, ::-1],
+                in1=sin_t[:, m : m + 1, :].to_broadcast(shape).rearrange("p h (i t) -> p h i t", t=2),
+                op=MULT,
+            )
+            nc.gpsimd.tensor_tensor(out=result[:], in0=direct[:], in1=crossed[:], op=ADD)
+            store(b, m, result[:], 0, HEADS_PER_TILE)
+
+        def copy_out(b, m, bank):
+            result = outp.tile([P, N_TILE], F32, name="result")
+            if m == 1:
+                nc.vector.tensor_copy(out=result[:], in_=bank[:])
+            else:
+                nc.scalar.copy(out=result[:], in_=bank[:])
+            store(b, m, result[:], 0, HEADS_PER_TILE)
+
+        banks = []
+        for m in range(M_TILES):
+            bank = psum.tile([P, N_TILE], F32, name="bank")
+            banks.append(bank)
+        for g in range(PASSES):
+            for m in range(M_TILES):
+                one_pass(banks[m], 0, m, g)
+        for m in range(M_TILES):
+            rotate(0, m, banks[m])
+
+        load_planes(w_planes[3], w_scales, *GROUPS[3])
+        for g in range(0, PASSES, 2):
+            load_w_codes(3, g, g + 2)
+
+        for b in range(1, BLOCKS):
+            for m in range(M_TILES):
+                if b == BLOCKS - 1 and m == M_TILES - 1:
+                    for half in range(2):
+                        bank = psum.tile([P, N_TILE], F32, name="bank")
+                        for g in range(PASSES):
+                            one_pass(bank, b, m, g, off=256 * half, width=256)
+                        result = outp.tile([P, N_TILE], F32, name="result")
+                        if half == 0:
+                            nc.scalar.copy(out=result[:, :256], in_=bank[:, :256])
+                        else:
+                            nc.vector.tensor_copy(out=result[:, :256], in_=bank[:, :256])
+                        store(b, m, result[:, :256], 2 * half, 2)
+                else:
+                    bank = psum.tile([P, N_TILE], F32, name="bank")
+                    for g in range(PASSES):
+                        one_pass(bank, b, m, g)
+                    if b < ROPE_BLOCKS:
+                        rotate(b, m, bank)
+                    else:
+                        copy_out(b, m, bank)

@@ -76,9 +76,7 @@ def tile_jointattention_pa_kernel(
         nc.vector.memset(x_planes[:].bitcast(I32), 0)
         nc.vector.memset(w_planes[0][:].bitcast(I32), 0)
         nc.vector.memset(w_planes[1][:].bitcast(I32), 0)
-        nc.gpsimd.dma_start(out=rope_raw[:], in_=rope[0].rearrange("(m p) d -> p m d", p=P))
-        nc.gpsimd.memset(w_planes[2][:].bitcast(I32), 0)
-        nc.gpsimd.memset(w_planes[3][:].bitcast(I32), 0)
+        nc.vector.memset(w_planes[2][:].bitcast(I32), 0)
         nc.scalar.copy(out=warm_out[:], in_=warm[:, 0:1])
 
         load_x_codes(0, 1)
@@ -89,6 +87,7 @@ def tile_jointattention_pa_kernel(
         load_w_codes(0, 1, 3)
         load_x_codes(3, 6)
         load_w_codes(0, 3, 6)
+        nc.sync.dma_start(out=rope_raw[:], in_=rope[0].rearrange("(m p) d -> p m d", p=P))
         for i in (1, 2):
             load_planes(w_planes[i], w_scales, *GROUPS[i])
             for g in range(0, PASSES, 2):
@@ -102,7 +101,7 @@ def tile_jointattention_pa_kernel(
         nc.vector.tensor_copy(out=sin_v[:, :, 1:2], in_=raw[:, :, 1:2])
 
         dummy = psum.tile([P, N_TILE], F32, name="bank")
-        for _ in range(12):
+        for _ in range(9):
             nc.tensor.matmul(dummy[:], lhsT=warm[:, :P], rhs=warm[:], start=True, stop=True)
 
         def one_pass(bank, b, m, g, off=0, width=N_TILE):
@@ -163,6 +162,7 @@ def tile_jointattention_pa_kernel(
         for m in range(M_TILES):
             rotate(0, m, banks[m])
 
+        nc.vector.memset(w_planes[3][:].bitcast(I32), 0)
         load_planes(w_planes[3], w_scales, *GROUPS[3])
         for g in range(0, PASSES, 2):
             load_w_codes(3, g, g + 2)

@@ -13,7 +13,8 @@ BLOCKS = COLS // N_TILE
 ROPE_BLOCKS = 6
 FLOPS = 2 * TOKENS * K * COLS
 
-GROUPS = ((0, 512), (512, 1024), (1536, 1536), (3072, 1536))
+GROUPS = ((0, 1024), (1024, 1024), (2048, 1024), (3072, 1536))
+FIRST_BLOCKS = 2
 
 F32 = mybir.dt.float32
 BF16 = mybir.dt.bfloat16
@@ -33,10 +34,12 @@ def tile_jointattention_pa_kernel(
     with ExitStack() as ctx:
         keep = ctx.enter_context(tc.tile_pool(name="keep", bufs=1))
         work = ctx.enter_context(tc.tile_pool(name="work", bufs=4))
-        outp = ctx.enter_context(tc.tile_pool(name="outp", bufs=12))
+        outp = ctx.enter_context(tc.tile_pool(name="outp", bufs=5))
         psum = ctx.enter_context(tc.psum_pool(name="psum", bufs=8))
         ctx.enter_context(tc.manual_schedule())
 
+        x_codes_raw = keep.tile([P, PASSES, 2 * TOKENS], U8, align_bytes=256, name="x_codes_raw")
+        x_planes_raw = keep.tile([P, PASSES, TOKENS], U8, align_bytes=256, name="x_planes_raw")
         x_codes = keep.tile([P, PASSES, 2 * TOKENS], U8, align_bytes=256, name="x_codes")
         x_planes = keep.tile([P, PASSES, TOKENS], U8, align_bytes=256, name="x_planes")
         w_codes = []
@@ -54,7 +57,7 @@ def tile_jointattention_pa_kernel(
 
         def load_x_codes(g0, g1):
             nc.sync.dma_start(
-                out=x_codes[:, g0:g1, :].bitcast(I32),
+                out=x_codes_raw[:, g0:g1, :].bitcast(I32),
                 in_=img_words[g0:g1].rearrange("g p n -> p g n").bitcast(I32),
             )
 
@@ -65,40 +68,52 @@ def tile_jointattention_pa_kernel(
                 in_=w_words[g0:g1, :, 2 * c0 : 2 * (c0 + width)].rearrange("g p n -> p g n").bitcast(I32),
             )
 
-        def load_planes(planes, scales, c0, width):
-            for q in range(4):
+        def load_planes(planes, scales, c0, width, g0=0, g1=PASSES):
+            for r in range(4):
                 nc.sync.dma_start(
-                    out=planes[32 * q : 32 * q + 4, :, :].bitcast(I32),
-                    in_=scales[:, 4 * q : 4 * q + 4, c0 : c0 + width].rearrange("g r n -> r g n").bitcast(I32),
+                    out=planes[r:P:32, g0:g1, :].bitcast(I32),
+                    in_=scales[g0:g1, r:16:4, c0 : c0 + width].rearrange("g q n -> q g n").bitcast(I32),
                 )
 
         nc.vector.memset(warm[:], 0.0)
-        nc.vector.memset(x_planes[:].bitcast(I32), 0)
+        nc.vector.memset(x_planes_raw[:].bitcast(I32), 0)
         nc.vector.memset(w_planes[0][:].bitcast(I32), 0)
-        nc.vector.memset(w_planes[1][:].bitcast(I32), 0)
-        nc.vector.memset(w_planes[2][:].bitcast(I32), 0)
         nc.scalar.copy(out=warm_out[:], in_=warm[:, 0:1])
 
         load_x_codes(0, 1)
         load_w_codes(0, 0, 1)
-        load_planes(x_planes, img_scales, 0, TOKENS)
-        load_planes(w_planes[0], w_scales, 0, GROUPS[0][1])
+        load_planes(x_planes_raw, img_scales, 0, TOKENS)
+        load_planes(w_planes[0], w_scales, *GROUPS[0])
         load_x_codes(1, 3)
-        load_w_codes(0, 1, 3)
+        load_w_codes(0, 1, 2)
+        load_w_codes(0, 2, 3)
         load_x_codes(3, 6)
-        load_w_codes(0, 3, 6)
-        nc.sync.dma_start(out=rope_raw[:], in_=rope[0].rearrange("(m p) d -> p m d", p=P))
-        for i in (1, 2):
-            load_planes(w_planes[i], w_scales, *GROUPS[i])
-            for g in range(0, PASSES, 2):
-                load_w_codes(i, g, g + 2)
-
+        load_w_codes(0, 3, 4)
+        load_w_codes(0, 4, 6)
+        nc.sync.dma_start(out=rope_raw[:], in_=rope[0].rearrange("(p m) d -> p m d", m=M_TILES))
+        for g in range(PASSES):
+            nc.vector.tensor_copy(
+                out=x_codes[:, g, :].rearrange("p (m n t) -> p m n t", m=M_TILES, t=2),
+                in_=x_codes_raw[:, g, :].rearrange("p (n m t) -> p m n t", m=M_TILES, t=2),
+            )
+            nc.vector.tensor_copy(
+                out=x_planes[:, g, :].rearrange("p (m n) -> p m n", m=M_TILES),
+                in_=x_planes_raw[:, g, :].rearrange("p (n m) -> p m n", m=M_TILES),
+            )
+            if g == 0:
+                nc.vector.memset(w_planes[1][:].bitcast(I32), 0)
         raw = rope_raw[:].rearrange("p m (i t) -> p (m i) t", t=2)
         cos_v = cos_t[:].rearrange("p m (i t) -> p (m i) t", t=2)
         sin_v = sin_t[:].rearrange("p m (i t) -> p (m i) t", t=2)
         nc.vector.tensor_copy(out=cos_v, in_=raw[:, :, 0:1].to_broadcast([P, M_TILES * D // 2, 2]))
         nc.vector.tensor_scalar(out=sin_v[:, :, 0:1], in0=raw[:, :, 1:2], scalar1=-1.0, scalar2=None, op0=MULT)
         nc.vector.tensor_copy(out=sin_v[:, :, 1:2], in_=raw[:, :, 1:2])
+        nc.vector.memset(w_planes[2][:].bitcast(I32), 0)
+
+        for i in (1, 2):
+            load_planes(w_planes[i], w_scales, *GROUPS[i])
+            for g in range(0, PASSES, 2):
+                load_w_codes(i, g, g + 2)
 
         dummy = psum.tile([P, N_TILE], F32, name="bank")
         for _ in range(9):
@@ -117,18 +132,24 @@ def tile_jointattention_pa_kernel(
                 stop=(g == PASSES - 1),
             )
 
-        def store(b, m, tile_ap, h_off, heads):
+        def store(b, results, h_off, heads):
             h0 = (b % 3) * HEADS_PER_TILE + h_off
             nc.sync.dma_start(
-                out=outs[b // 3][0, h0 : h0 + heads, P * m : P * (m + 1), :].rearrange("h n d -> n h d"),
-                in_=tile_ap.rearrange("p (h d) -> p h d", d=D),
+                out=outs[b // 3][0, h0 : h0 + heads].rearrange("h (p m) d -> p h m d", m=M_TILES),
+                in_=results[:, h_off : h_off + heads],
             )
 
-        def rotate(b, m, bank):
+        def store_one(b, m, results, h_off, heads):
+            h0 = (b % 3) * HEADS_PER_TILE + h_off
+            nc.sync.dma_start(
+                out=outs[b // 3][0, h0 : h0 + heads].rearrange("h (p m) d -> p h m d", m=M_TILES)[:, :, m],
+                in_=results.rearrange("p (h d) -> p h d", d=D),
+            )
+
+        def rotate(m, bank, results):
             shape = [P, HEADS_PER_TILE, D]
             direct = work.tile([P, N_TILE], F32, name="direct")
             crossed = work.tile([P, N_TILE], F32, name="crossed")
-            result = outp.tile([P, N_TILE], F32, name="result")
             nc.vector.tensor_tensor(
                 out=direct[:].rearrange("p (h d) -> p h d", d=D),
                 in0=bank[:].rearrange("p (h d) -> p h d", d=D),
@@ -141,50 +162,58 @@ def tile_jointattention_pa_kernel(
                 in1=sin_t[:, m : m + 1, :].to_broadcast(shape).rearrange("p h (i t) -> p h i t", t=2),
                 op=MULT,
             )
-            nc.gpsimd.tensor_tensor(out=result[:], in0=direct[:], in1=crossed[:], op=ADD)
-            store(b, m, result[:], 0, HEADS_PER_TILE)
+            nc.gpsimd.tensor_tensor(
+                out=results[:, :, m],
+                in0=direct[:].rearrange("p (h d) -> p h d", d=D),
+                in1=crossed[:].rearrange("p (h d) -> p h d", d=D),
+                op=ADD,
+            )
 
-        def copy_out(b, m, bank):
-            result = outp.tile([P, N_TILE], F32, name="result")
-            if m == 1:
-                nc.vector.tensor_copy(out=result[:], in_=bank[:])
-            else:
-                nc.scalar.copy(out=result[:], in_=bank[:])
-            store(b, m, result[:], 0, HEADS_PER_TILE)
-
-        banks = []
-        for m in range(M_TILES):
-            bank = psum.tile([P, N_TILE], F32, name="bank")
-            banks.append(bank)
-        for g in range(PASSES):
+        first_banks = {}
+        for b in range(FIRST_BLOCKS):
             for m in range(M_TILES):
-                one_pass(banks[m], 0, m, g)
-        for m in range(M_TILES):
-            rotate(0, m, banks[m])
+                bank = psum.tile([P, N_TILE], F32, name="bank")
+                first_banks[b, m] = bank
+        for g in range(PASSES):
+            for b in range(FIRST_BLOCKS):
+                for m in range(M_TILES):
+                    one_pass(first_banks[b, m], b, m, g)
+        for b in range(FIRST_BLOCKS):
+            results = outp.tile([P, HEADS_PER_TILE, M_TILES, D], F32, name="results")
+            for m in range(M_TILES):
+                rotate(m, first_banks[b, m], results)
+            store(b, results, 0, HEADS_PER_TILE)
 
         nc.vector.memset(w_planes[3][:].bitcast(I32), 0)
         load_planes(w_planes[3], w_scales, *GROUPS[3])
         for g in range(0, PASSES, 2):
             load_w_codes(3, g, g + 2)
 
-        for b in range(1, BLOCKS):
+        for b in range(FIRST_BLOCKS, BLOCKS - 1):
+            results = outp.tile([P, HEADS_PER_TILE, M_TILES, D], F32, name="results")
             for m in range(M_TILES):
-                if b == BLOCKS - 1 and m == M_TILES - 1:
-                    for half in range(2):
-                        bank = psum.tile([P, N_TILE], F32, name="bank")
-                        for g in range(PASSES):
-                            one_pass(bank, b, m, g, off=256 * half, width=256)
-                        result = outp.tile([P, N_TILE], F32, name="result")
-                        if half == 0:
-                            nc.scalar.copy(out=result[:, :256], in_=bank[:, :256])
-                        else:
-                            nc.vector.tensor_copy(out=result[:, :256], in_=bank[:, :256])
-                        store(b, m, result[:, :256], 2 * half, 2)
+                bank = psum.tile([P, N_TILE], F32, name="bank")
+                for g in range(PASSES):
+                    one_pass(bank, b, m, g)
+                if b < ROPE_BLOCKS:
+                    rotate(m, bank, results)
+                elif m == 1:
+                    nc.vector.tensor_copy(out=results[:, :, m], in_=bank[:].rearrange("p (h d) -> p h d", d=D))
                 else:
-                    bank = psum.tile([P, N_TILE], F32, name="bank")
-                    for g in range(PASSES):
-                        one_pass(bank, b, m, g)
-                    if b < ROPE_BLOCKS:
-                        rotate(b, m, bank)
-                    else:
-                        copy_out(b, m, bank)
+                    nc.scalar.copy(out=results[:, :, m], in_=bank[:].rearrange("p (h d) -> p h d", d=D))
+            store(b, results, 0, HEADS_PER_TILE)
+
+        b = BLOCKS - 1
+        for m in range(M_TILES):
+            pieces = 2 if m == M_TILES - 1 else 1
+            width = N_TILE // pieces
+            for piece in range(pieces):
+                bank = psum.tile([P, N_TILE], F32, name="bank")
+                for g in range(PASSES):
+                    one_pass(bank, b, m, g, off=width * piece, width=width)
+                last = work.tile([P, N_TILE], F32, name="last")
+                if (m + piece) % 2 == 1:
+                    nc.vector.tensor_copy(out=last[:, :width], in_=bank[:, :width])
+                else:
+                    nc.scalar.copy(out=last[:, :width], in_=bank[:, :width])
+                store_one(b, m, last[:, :width], HEADS_PER_TILE // pieces * piece, HEADS_PER_TILE // pieces)

from contextlib import ExitStack

import concourse.mybir as mybir

P = 128
TOKENS, K, COLS = 384, 3072, 4608
HEADS, D = 12, 128
PASSES = K // 512
M_TILES = TOKENS // P
N_TILE = 512
HEADS_PER_TILE = N_TILE // D
BLOCKS = COLS // N_TILE
ROPE_BLOCKS = 6
FLOPS = 2 * TOKENS * K * COLS

GROUPS = ((0, 1024), (1024, 1024), (2048, 1024), (3072, 1536))
FIRST_BLOCKS = 2

F32 = mybir.dt.float32
BF16 = mybir.dt.bfloat16
I32 = mybir.dt.int32
U8 = mybir.dt.uint8
FP4X4 = mybir.dt.float4_e2m1fn_x4
MULT = mybir.AluOpType.mult
ADD = mybir.AluOpType.add


def tile_jointattention_pa_kernel(
    tc, img_words, img_scales, rope, w_words, w_scales, out_q, out_k, out_v
):
    nc = tc.nc
    outs = (out_q, out_k, out_v)

    with ExitStack() as ctx:
        keep = ctx.enter_context(tc.tile_pool(name="keep", bufs=1))
        work = ctx.enter_context(tc.tile_pool(name="work", bufs=4))
        outp = ctx.enter_context(tc.tile_pool(name="outp", bufs=5))
        psum = ctx.enter_context(tc.psum_pool(name="psum", bufs=8))
        ctx.enter_context(tc.manual_schedule())

        x_codes_raw = keep.tile([P, PASSES, 2 * TOKENS], U8, align_bytes=256, name="x_codes_raw")
        x_planes_raw = keep.tile([P, PASSES, TOKENS], U8, align_bytes=256, name="x_planes_raw")
        x_codes = keep.tile([P, PASSES, 2 * TOKENS], U8, align_bytes=256, name="x_codes")
        x_planes = keep.tile([P, PASSES, TOKENS], U8, align_bytes=256, name="x_planes")
        w_codes = []
        w_planes = []
        for i, (c0, width) in enumerate(GROUPS):
            codes = keep.tile([P, PASSES, 2 * width], U8, align_bytes=256, name=f"w_codes{i}")
            planes = keep.tile([P, PASSES, width], U8, align_bytes=256, name=f"w_planes{i}")
            w_codes.append(codes)
            w_planes.append(planes)
        warm = keep.tile([P, N_TILE], BF16, name="warm")
        warm_out = keep.tile([P, 1], BF16, name="warm_out")
        rope_raw = keep.tile([P, M_TILES, D], BF16, name="rope_raw")
        cos_t = keep.tile([P, M_TILES, D], F32, name="cos_t")
        sin_t = keep.tile([P, M_TILES, D], F32, name="sin_t")

        def load_x_codes(g0, g1):
            nc.sync.dma_start(
                out=x_codes_raw[:, g0:g1, :].bitcast(I32),
                in_=img_words[g0:g1].rearrange("g p n -> p g n").bitcast(I32),
            )

        def load_w_codes(i, g0, g1):
            c0, width = GROUPS[i]
            nc.sync.dma_start(
                out=w_codes[i][:, g0:g1, :].bitcast(I32),
                in_=w_words[g0:g1, :, 2 * c0 : 2 * (c0 + width)].rearrange("g p n -> p g n").bitcast(I32),
            )

        def load_planes(planes, scales, c0, width, g0=0, g1=PASSES):
            for r in range(4):
                nc.sync.dma_start(
                    out=planes[r:P:32, g0:g1, :].bitcast(I32),
                    in_=scales[g0:g1, r:16:4, c0 : c0 + width].rearrange("g q n -> q g n").bitcast(I32),
                )

        nc.vector.memset(warm[:], 0.0)
        nc.vector.memset(x_planes_raw[:].bitcast(I32), 0)
        nc.vector.memset(w_planes[0][:].bitcast(I32), 0)
        nc.scalar.copy(out=warm_out[:], in_=warm[:, 0:1])

        load_x_codes(0, 1)
        load_w_codes(0, 0, 1)
        load_planes(x_planes_raw, img_scales, 0, TOKENS)
        load_planes(w_planes[0], w_scales, *GROUPS[0])
        load_x_codes(1, 3)
        load_w_codes(0, 1, 2)
        load_w_codes(0, 2, 3)
        load_x_codes(3, 6)
        load_w_codes(0, 3, 4)
        load_w_codes(0, 4, 6)
        nc.sync.dma_start(out=rope_raw[:], in_=rope[0].rearrange("(p m) d -> p m d", m=M_TILES))
        for g in range(PASSES):
            nc.vector.tensor_copy(
                out=x_codes[:, g, :].rearrange("p (m n t) -> p m n t", m=M_TILES, t=2),
                in_=x_codes_raw[:, g, :].rearrange("p (n m t) -> p m n t", m=M_TILES, t=2),
            )
            nc.vector.tensor_copy(
                out=x_planes[:, g, :].rearrange("p (m n) -> p m n", m=M_TILES),
                in_=x_planes_raw[:, g, :].rearrange("p (n m) -> p m n", m=M_TILES),
            )
            if g == 0:
                nc.vector.memset(w_planes[1][:].bitcast(I32), 0)
        raw = rope_raw[:].rearrange("p m (i t) -> p (m i) t", t=2)
        cos_v = cos_t[:].rearrange("p m (i t) -> p (m i) t", t=2)
        sin_v = sin_t[:].rearrange("p m (i t) -> p (m i) t", t=2)
        nc.vector.tensor_copy(out=cos_v, in_=raw[:, :, 0:1].to_broadcast([P, M_TILES * D // 2, 2]))
        nc.vector.tensor_scalar(out=sin_v[:, :, 0:1], in0=raw[:, :, 1:2], scalar1=-1.0, scalar2=None, op0=MULT)
        nc.vector.tensor_copy(out=sin_v[:, :, 1:2], in_=raw[:, :, 1:2])
        nc.vector.memset(w_planes[2][:].bitcast(I32), 0)

        for i in (1, 2):
            load_planes(w_planes[i], w_scales, *GROUPS[i])
            for g in range(0, PASSES, 2):
                load_w_codes(i, g, g + 2)

        dummy = psum.tile([P, N_TILE], F32, name="bank")
        for _ in range(9):
            nc.tensor.matmul(dummy[:], lhsT=warm[:, :P], rhs=warm[:], start=True, stop=True)

        def one_pass(bank, b, m, g, off=0, width=N_TILE):
            i = max(j for j, (c0, w) in enumerate(GROUPS) if c0 <= b * N_TILE)
            c = b * N_TILE - GROUPS[i][0] + off
            nc.tensor.matmul_mx(
                out=bank[:, :width],
                lhsT=x_codes[:, g, 2 * P * m : 2 * P * (m + 1)].bitcast(FP4X4),
                lhsT_scale=x_planes[:, g, P * m : P * (m + 1)],
                rhs=w_codes[i][:, g, 2 * c : 2 * (c + width)].bitcast(FP4X4),
                rhs_scale=w_planes[i][:, g, c : c + width],
                start=(g == 0),
                stop=(g == PASSES - 1),
            )

        def store(b, results, h_off, heads):
            h0 = (b % 3) * HEADS_PER_TILE + h_off
            nc.sync.dma_start(
                out=outs[b // 3][0, h0 : h0 + heads].rearrange("h (p m) d -> p h m d", m=M_TILES),
                in_=results[:, h_off : h_off + heads],
            )

        def store_one(b, m, results, h_off, heads):
            h0 = (b % 3) * HEADS_PER_TILE + h_off
            nc.sync.dma_start(
                out=outs[b // 3][0, h0 : h0 + heads].rearrange("h (p m) d -> p h m d", m=M_TILES)[:, :, m],
                in_=results.rearrange("p (h d) -> p h d", d=D),
            )

        def rotate(m, bank, results):
            shape = [P, HEADS_PER_TILE, D]
            direct = work.tile([P, N_TILE], F32, name="direct")
            crossed = work.tile([P, N_TILE], F32, name="crossed")
            nc.vector.tensor_tensor(
                out=direct[:].rearrange("p (h d) -> p h d", d=D),
                in0=bank[:].rearrange("p (h d) -> p h d", d=D),
                in1=cos_t[:, m : m + 1, :].to_broadcast(shape),
                op=MULT,
            )
            nc.vector.tensor_tensor(
                out=crossed[:].rearrange("p (h i t) -> p h i t", t=2, i=D // 2),
                in0=bank[:].rearrange("p (h i t) -> p h i t", t=2, i=D // 2)[:, :, :, ::-1],
                in1=sin_t[:, m : m + 1, :].to_broadcast(shape).rearrange("p h (i t) -> p h i t", t=2),
                op=MULT,
            )
            nc.gpsimd.tensor_tensor(
                out=results[:, :, m],
                in0=direct[:].rearrange("p (h d) -> p h d", d=D),
                in1=crossed[:].rearrange("p (h d) -> p h d", d=D),
                op=ADD,
            )

        first_banks = {}
        for b in range(FIRST_BLOCKS):
            for m in range(M_TILES):
                bank = psum.tile([P, N_TILE], F32, name="bank")
                first_banks[b, m] = bank
        for g in range(PASSES):
            for b in range(FIRST_BLOCKS):
                for m in range(M_TILES):
                    one_pass(first_banks[b, m], b, m, g)
        for b in range(FIRST_BLOCKS):
            results = outp.tile([P, HEADS_PER_TILE, M_TILES, D], F32, name="results")
            for m in range(M_TILES):
                rotate(m, first_banks[b, m], results)
            store(b, results, 0, HEADS_PER_TILE)

        nc.vector.memset(w_planes[3][:].bitcast(I32), 0)
        load_planes(w_planes[3], w_scales, *GROUPS[3])
        for g in range(0, PASSES, 2):
            load_w_codes(3, g, g + 2)

        for b in range(FIRST_BLOCKS, BLOCKS - 1):
            results = outp.tile([P, HEADS_PER_TILE, M_TILES, D], F32, name="results")
            for m in range(M_TILES):
                bank = psum.tile([P, N_TILE], F32, name="bank")
                for g in range(PASSES):
                    one_pass(bank, b, m, g)
                if b < ROPE_BLOCKS:
                    rotate(m, bank, results)
                elif m == 1:
                    nc.vector.tensor_copy(out=results[:, :, m], in_=bank[:].rearrange("p (h d) -> p h d", d=D))
                else:
                    nc.scalar.copy(out=results[:, :, m], in_=bank[:].rearrange("p (h d) -> p h d", d=D))
            store(b, results, 0, HEADS_PER_TILE)

        b = BLOCKS - 1
        for m in range(M_TILES):
            pieces = 2 if m == M_TILES - 1 else 1
            width = N_TILE // pieces
            for piece in range(pieces):
                bank = psum.tile([P, N_TILE], F32, name="bank")
                for g in range(PASSES):
                    one_pass(bank, b, m, g, off=width * piece, width=width)
                last = work.tile([P, N_TILE], F32, name="last")
                if (m + piece) % 2 == 1:
                    nc.vector.tensor_copy(out=last[:, :width], in_=bank[:, :width])
                else:
                    nc.scalar.copy(out=last[:, :width], in_=bank[:, :width])
                store_one(b, m, last[:, :width], HEADS_PER_TILE // pieces * piece, HEADS_PER_TILE // pieces)
